import numpy as np
import ml_dtypes


def mxq(x, axis, fmt="e4m3"):
    dtype, down = {"e4m3": (ml_dtypes.float8_e4m3fn, 7), "e5m2": (ml_dtypes.float8_e5m2, 14)}[fmt]
    v = np.moveaxis(np.asarray(x, np.float32).astype(ml_dtypes.bfloat16).astype(np.float64), axis, -1)
    blocks = v.reshape(v.shape[:-1] + (-1, 32))
    amax = np.abs(blocks).max(-1, keepdims=True)
    byte = np.maximum(np.where(amax > 0, np.frexp(amax)[1] - 1 + 127, 0) - down, 1)
    scale = np.exp2(byte - 127.0)
    codes = (blocks / scale).astype(np.float32).astype(dtype).astype(np.float64)
    return np.moveaxis((codes * scale).reshape(v.shape), -1, axis)


WIDE = False


def mx_kscale(k):
    if not WIDE:
        return np.ones(k)
    levels = np.array([10, -10, 5, -5, 0])
    a = np.random.permutation(np.resize(levels, k // 512 * 4)).reshape(k // 512, 4)
    idx = np.arange(k)
    return np.exp2(a[idx // 512, idx % 128 // 32])


BF16 = ml_dtypes.bfloat16


def bf(x):
    return np.asarray(x, np.float32).astype(BF16)


def f64(x):
    return np.asarray(x).astype(np.float64)


T, B, D, M = 128, 128, 512, 128
TEMP = 0.1
QS = 0.3
SC = 2.0
MS = SC * TEMP / (QS * np.sqrt(D))
WS = QS * np.sqrt(SC**2 / D + 0.4 / B)


def sigmoid(v):
    return 1.0 / (1.0 + np.exp(-v))


def setup_inputs():
    s = mx_kscale(D)
    return {"queries": bf(np.random.standard_normal((T, B, D)) * QS / s),
            "memory_items": bf(np.random.standard_normal((M, D)) * MS * s),
            "wq": bf(np.random.standard_normal((M, D)) * WS * s),
            "U_w": bf(np.random.standard_normal((D, D)) / (MS * np.sqrt(D)) / s[None, :]),
            "W_w": bf(np.random.standard_normal((D, D)) / (WS * np.sqrt(D)) / s[None, :])}


def reference(queries, memory_items, wq, U_w, W_w):
    q = f64(queries).reshape(T * B, D)
    mem = f64(memory_items)
    w = f64(wq)
    gate = sigmoid((mxq(mem, 1, "e4m3") @ mxq(f64(U_w), 1, "e4m3").T) + (mxq(w, 1, "e4m3") @ mxq(f64(W_w), 1, "e4m3").T))
    m_new = (1.0 - gate) * mem + gate * w
    logits = (mxq(q, 1, "e4m3") @ mxq(m_new, 1, "e4m3").T) / TEMP
    e = np.exp(logits - logits.max(-1, keepdims=True))
    w_att = e / e.sum(-1, keepdims=True)
    return m_new, w_att.reshape(T, B, M)

@@ -1,0 +1,201 @@
+from contextlib import ExitStack
+
+import concourse.mybir as mybir
+from concourse.masks import make_identity
+
+F32 = mybir.dt.float32
+BF16 = mybir.dt.bfloat16
+U32 = mybir.dt.uint32
+U8 = mybir.dt.uint8
+FP8X4 = mybir.dt.float8_e4m3fn_x4
+ACT = mybir.ActivationFunctionType
+ALU = mybir.AluOpType
+AXIS = mybir.AxisListType
+
+P = 128
+D = 512
+SLOTS = 128
+ROWS = 128 * 128
+INV_TEMP = 1.0 / 0.1
+PACK = 4
+HALVES = 2
+ROW_TILES = ROWS // P
+BANK_TILES = 2
+GROUP = 4
+CHUNK = 8
+GATE_COPY_EVERY = 2
+QUERY_COPY_EVERY = 6
+
+FLOPS = 2 * (2 * SLOTS * D * D + ROWS * D * SLOTS)
+
+
+def transpose_and_quantise(nc, banks, stage, identity, row_tiles, first_bank, vector_every, codes, scales):
+    grouped = stage.tile([P, len(row_tiles) * P * PACK], BF16, tag="grouped", align_bytes=64)
+    grouped_words = grouped[:].bitcast(F32).rearrange("p (c u) -> p c u", u=HALVES)
+    for b in range(len(row_tiles) // BANK_TILES):
+        flipped = banks.tile([P, HALVES, BANK_TILES * P], F32, tag="flipped")
+        for i in range(BANK_TILES):
+            words = row_tiles[b * BANK_TILES + i].bitcast(F32)
+            for u in range(HALVES):
+                nc.tensor.transpose(flipped[:, u, i * P : (i + 1) * P], words[:, u * P : (u + 1) * P], identity)
+        bank_columns = slice(b * BANK_TILES * P, (b + 1) * BANK_TILES * P)
+        if (first_bank + b) % vector_every == 0:
+            nc.vector.tensor_copy(out=grouped_words[:, bank_columns, :], in_=flipped[:].rearrange("p u c -> p c u"))
+        else:
+            nc.scalar.copy(out=grouped_words[:, bank_columns, :], in_=flipped[:].rearrange("p u c -> p c u"))
+    nc.vector.quantize_mx(out=codes.bitcast(FP8X4), scales=scales, in_=grouped[:])
+
+
+def tile_gatedmemorymodule_pb_kernel(tc, queries, memory_items, wq, U_w, W_w, out_0, out_1):
+    nc = tc.nc
+    query_rows = queries.flatten_outer_dims().rearrange("(p t) d -> p t d", p=P)
+    att_rows = out_1.flatten_outer_dims().rearrange("(p t) m -> p t m", p=P)
+
+    with ExitStack() as ctx:
+        keep = ctx.enter_context(tc.tile_pool(name="keep", bufs=1))
+        query_pool = ctx.enter_context(tc.tile_pool(name="query", bufs=ROW_TILES // CHUNK))
+        stage = ctx.enter_context(tc.tile_pool(name="stage", bufs=3))
+        packed = ctx.enter_context(tc.tile_pool(name="packed", bufs=8))
+        stats = ctx.enter_context(tc.tile_pool(name="stats", bufs=4))
+        att_pool = ctx.enter_context(tc.tile_pool(name="att", bufs=4))
+        banks = ctx.enter_context(tc.psum_pool(name="banks", bufs=4))
+        logit_banks = ctx.enter_context(tc.psum_pool(name="logit_banks", bufs=3))
+        gate_bank = ctx.enter_context(tc.psum_pool(name="gate_bank", bufs=1))
+
+        mem_raw = keep.tile([P, D], BF16)
+        nc.sync.dma_start(out=mem_raw[:], in_=memory_items)
+        wq_raw = keep.tile([P, D], BF16)
+        nc.sync.dma_start(out=wq_raw[:], in_=wq)
+        u_raw = keep.tile([P, D // P, D], BF16)
+        nc.sync.dma_start(out=u_raw[:], in_=U_w.rearrange("(i p) k -> p i k", p=P))
+        w_raw = keep.tile([P, D // P, D], BF16)
+        nc.sync.dma_start(out=w_raw[:], in_=W_w.rearrange("(i p) k -> p i k", p=P))
+        query_chunks = []
+        for c in range(ROW_TILES // CHUNK):
+            query_raw = query_pool.tile([P, CHUNK, D], BF16)
+            nc.sync.dma_start(out=query_raw[:], in_=query_rows[:, c * CHUNK : (c + 1) * CHUNK, :])
+            query_chunks.append(query_raw)
+
+        identity = keep.tile([P, P], F32)
+        make_identity(nc, identity[:])
+        scratch_in = keep.tile([P, 1], F32)
+        nc.vector.memset(scratch_in[:], 0.0)
+        scratch_out = keep.tile([P, 1], F32)
+        nc.scalar.activation(out=scratch_out[:], in_=scratch_in[:], func=ACT.Exp)
+
+        slot_codes = keep.tile([P, 2 * SLOTS], U32, align_bytes=64)
+        slot_scales = keep.tile([P, 2 * SLOTS], U8, align_bytes=64)
+        transpose_and_quantise(
+            nc, banks, stage, identity[:], [mem_raw[:], wq_raw[:]], 0, GATE_COPY_EVERY, slot_codes[:], slot_scales[:]
+        )
+        u_codes = keep.tile([P, D], U32, align_bytes=64)
+        u_scales = keep.tile([P, D], U8, align_bytes=64)
+        transpose_and_quantise(
+            nc, banks, stage, identity[:], [u_raw[:, i, :] for i in range(D // P)], 1, GATE_COPY_EVERY, u_codes[:], u_scales[:]
+        )
+        w_codes = keep.tile([P, D], U32, align_bytes=64)
+        w_scales = keep.tile([P, D], U8, align_bytes=64)
+        transpose_and_quantise(
+            nc, banks, stage, identity[:], [w_raw[:, i, :] for i in range(D // P)], 1, GATE_COPY_EVERY, w_codes[:], w_scales[:]
+        )
+        slot_sum = keep.tile([P, D], F32)
+        nc.vector.tensor_tensor(out=slot_sum[:], in0=wq_raw[:], in1=mem_raw[:], op=ALU.add)
+        slot_diff = keep.tile([P, D], F32)
+        nc.vector.tensor_tensor(out=slot_diff[:], in0=wq_raw[:], in1=mem_raw[:], op=ALU.subtract)
+
+        gate_sum = gate_bank.tile([P, D], F32, tag="gate_bank")
+        nc.tensor.matmul_mx(
+            out=gate_sum[:],
+            lhsT=slot_codes[:, 0:SLOTS].bitcast(FP8X4),
+            lhsT_scale=slot_scales[:, 0:SLOTS],
+            rhs=u_codes[:].bitcast(FP8X4),
+            rhs_scale=u_scales[:],
+            start=True,
+            stop=False,
+        )
+        nc.tensor.matmul_mx(
+            out=gate_sum[:],
+            lhsT=slot_codes[:, SLOTS : 2 * SLOTS].bitcast(FP8X4),
+            lhsT_scale=slot_scales[:, SLOTS : 2 * SLOTS],
+            rhs=w_codes[:].bitcast(FP8X4),
+            rhs_scale=w_scales[:],
+            start=False,
+            stop=True,
+        )
+        tanh_half = keep.tile([P, D], F32)
+        nc.scalar.activation(out=tanh_half[:], in_=gate_sum[:], func=ACT.Tanh, scale=0.5)
+        swing = keep.tile([P, D], F32)
+        nc.vector.scalar_tensor_tensor(
+            out=swing[:], in0=tanh_half[:], scalar=0.5, in1=slot_diff[:], op0=ALU.mult, op1=ALU.mult
+        )
+        m_new = keep.tile([P, D], F32)
+        nc.vector.scalar_tensor_tensor(
+            out=m_new[:], in0=slot_sum[:], scalar=0.5, in1=swing[:], op0=ALU.mult, op1=ALU.add
+        )
+        nc.sync.dma_start(out=out_0, in_=m_new[:])
+
+        m_features = m_new[:].rearrange("s (u p e) -> s u e p", u=HALVES, e=2)
+        m_flipped = gate_bank.tile([P, PACK, SLOTS], F32, tag="gate_bank")
+        for u in range(HALVES):
+            for e in range(2):
+                nc.tensor.transpose(m_flipped[:, 2 * u + e, :], m_features[:, u, e, :], identity[:])
+        m_grouped = keep.tile([P, SLOTS, PACK], BF16, align_bytes=64)
+        nc.vector.tensor_copy(out=m_grouped[:], in_=m_flipped[:].rearrange("p t s -> p s t"))
+        m_codes = keep.tile([P, SLOTS], U32, align_bytes=64)
+        m_scales = keep.tile([P, SLOTS], U8, align_bytes=64)
+        nc.vector.quantize_mx(
+            out=m_codes[:].bitcast(FP8X4), scales=m_scales[:], in_=m_grouped[:].rearrange("p s t -> p (s t)")
+        )
+
+        for c in range(ROW_TILES // CHUNK):
+            att = att_pool.tile([P, CHUNK, SLOTS], F32)
+            for first in range(0, CHUNK, GROUP):
+                query_codes = packed.tile([P, GROUP * P], U32, align_bytes=64)
+                query_scales = packed.tile([P, GROUP * P], U8, align_bytes=64)
+                transpose_and_quantise(
+                    nc,
+                    banks,
+                    stage,
+                    identity[:],
+                    [query_chunks[c][:, first + i, :] for i in range(GROUP)],
+                    (c * CHUNK + first) // BANK_TILES,
+                    QUERY_COPY_EVERY,
+                    query_codes[:],
+                    query_scales[:],
+                )
+                logits = logit_banks.tile([P, GROUP, SLOTS], F32)
+                for i in range(GROUP):
+                    nc.tensor.matmul_mx(
+                        out=logits[:, i, :],
+                        lhsT=query_codes[:, i * P : (i + 1) * P].bitcast(FP8X4),
+                        lhsT_scale=query_scales[:, i * P : (i + 1) * P],
+                        rhs=m_codes[:].bitcast(FP8X4),
+                        rhs_scale=m_scales[:],
+                        start=True,
+                        stop=True,
+                    )
+                row_max = stats.tile([P, GROUP], F32)
+                nc.vector.tensor_reduce(out=row_max[:], in_=logits[:], axis=AXIS.X, op=ALU.max)
+                shift = stats.tile([P, GROUP], F32)
+                nc.vector.tensor_scalar(out=shift[:], in0=row_max[:], scalar1=-INV_TEMP, scalar2=None, op0=ALU.mult)
+                row_sum = stats.tile([P, GROUP], F32)
+                for i in range(GROUP):
+                    nc.scalar.activation(
+                        out=att[:, first + i, :],
+                        in_=logits[:, i, :],
+                        func=ACT.Exp,
+                        bias=shift[:, i : i + 1],
+                        scale=INV_TEMP,
+                        accum_out=row_sum[:, i : i + 1],
+                    )
+                inv_sum = stats.tile([P, GROUP], F32)
+                nc.vector.reciprocal(out=inv_sum[:], in_=row_sum[:])
+                for i in range(GROUP):
+                    nc.vector.tensor_scalar(
+                        out=att[:, first + i, :],
+                        in0=att[:, first + i, :],
+                        scalar1=inv_sum[:, i : i + 1],
+                        scalar2=None,
+                        op0=ALU.mult,
+                    )
+            nc.sync.dma_start(out=att_rows[:, c * CHUNK : (c + 1) * CHUNK, :], in_=att[:])

@@ -60,7 +60,7 @@ def tile_gatedmemorymodule_pb_kernel(tc, queries, memory_items, wq, U_w, W_w, ou
         att_pool = ctx.enter_context(tc.tile_pool(name="att", bufs=4))
         banks = ctx.enter_context(tc.psum_pool(name="banks", bufs=4))
         logit_banks = ctx.enter_context(tc.psum_pool(name="logit_banks", bufs=3))
-        gate_bank = ctx.enter_context(tc.psum_pool(name="gate_bank", bufs=1))
+        clock_bank = ctx.enter_context(tc.psum_pool(name="clock_bank", bufs=1))
 
         mem_raw = keep.tile([P, D], BF16)
         nc.sync.dma_start(out=mem_raw[:], in_=memory_items)
@@ -103,7 +103,7 @@ def tile_gatedmemorymodule_pb_kernel(tc, queries, memory_items, wq, U_w, W_w, ou
         slot_diff = keep.tile([P, D], F32)
         nc.vector.tensor_tensor(out=slot_diff[:], in0=wq_raw[:], in1=mem_raw[:], op=ALU.subtract)
 
-        gate_sum = gate_bank.tile([P, D], F32, tag="gate_bank")
+        gate_sum = logit_banks.tile([P, D], F32, tag="logits")
         nc.tensor.matmul_mx(
             out=gate_sum[:],
             lhsT=slot_codes[:, 0:SLOTS].bitcast(FP8X4),
@@ -135,7 +135,7 @@ def tile_gatedmemorymodule_pb_kernel(tc, queries, memory_items, wq, U_w, W_w, ou
         nc.sync.dma_start(out=out_0, in_=m_new[:])
 
         m_features = m_new[:].rearrange("s (u p e) -> s u e p", u=HALVES, e=2)
-        m_flipped = gate_bank.tile([P, PACK, SLOTS], F32, tag="gate_bank")
+        m_flipped = logit_banks.tile([P, PACK, SLOTS], F32, tag="logits")
         for u in range(HALVES):
             for e in range(2):
                 nc.tensor.transpose(m_flipped[:, 2 * u + e, :], m_features[:, u, e, :], identity[:])
@@ -163,7 +163,17 @@ def tile_gatedmemorymodule_pb_kernel(tc, queries, memory_items, wq, U_w, W_w, ou
                     query_codes[:],
                     query_scales[:],
                 )
-                logits = logit_banks.tile([P, GROUP, SLOTS], F32)
+                unread = clock_bank.tile([P, D], F32)
+                nc.tensor.matmul_mx(
+                    out=unread[:],
+                    lhsT=slot_codes[:, 0:SLOTS].bitcast(FP8X4),
+                    lhsT_scale=slot_scales[:, 0:SLOTS],
+                    rhs=u_codes[:].bitcast(FP8X4),
+                    rhs_scale=u_scales[:],
+                    start=True,
+                    stop=True,
+                )
+                logits = logit_banks.tile([P, GROUP, SLOTS], F32, tag="logits")
                 for i in range(GROUP):
                     nc.tensor.matmul_mx(
                         out=logits[:, i, :],

@@ -19,31 +19,46 @@ ROWS = 128 * 128
 INV_TEMP = 1.0 / 0.1
 PACK = 4
 HALVES = 2
-ROW_TILES = ROWS // P
 BANK_TILES = 2
 GROUP = 4
 CHUNK = 8
+GROUPS = ROWS // P // GROUP
+CHUNK_GROUPS = CHUNK // GROUP
 GATE_COPY_EVERY = 2
 QUERY_COPY_EVERY = 6
+
+GATHER_LAG = 1
+QUANTISE_LAG = 2
+SCORE_LAG = 6
+MAX_LAG = SCORE_LAG + 1
+EXP_LAG = SCORE_LAG + 2
+NORMALISE_LAG = SCORE_LAG + 3
 
 FLOPS = 2 * (2 * SLOTS * D * D + ROWS * D * SLOTS)
 
 
-def transpose_and_quantise(nc, banks, stage, identity, row_tiles, first_bank, vector_every, codes, scales):
-    grouped = stage.tile([P, len(row_tiles) * P * PACK], BF16, tag="grouped", align_bytes=64)
-    grouped_words = grouped[:].bitcast(F32).rearrange("p (c u) -> p c u", u=HALVES)
+def flip_rows(nc, banks, identity, row_tiles):
+    filled = []
     for b in range(len(row_tiles) // BANK_TILES):
         flipped = banks.tile([P, HALVES, BANK_TILES * P], F32, tag="flipped")
         for i in range(BANK_TILES):
             words = row_tiles[b * BANK_TILES + i].bitcast(F32)
             for u in range(HALVES):
                 nc.tensor.transpose(flipped[:, u, i * P : (i + 1) * P], words[:, u * P : (u + 1) * P], identity)
+        filled.append(flipped)
+    return filled
+
+
+def gather_words(nc, stage, filled, first_bank, vector_every):
+    grouped = stage.tile([P, len(filled) * BANK_TILES * P * PACK], BF16, tag="grouped", align_bytes=64)
+    grouped_words = grouped[:].bitcast(F32).rearrange("p (c u) -> p c u", u=HALVES)
+    for b in range(len(filled)):
         bank_columns = slice(b * BANK_TILES * P, (b + 1) * BANK_TILES * P)
         if (first_bank + b) % vector_every == 0:
-            nc.vector.tensor_copy(out=grouped_words[:, bank_columns, :], in_=flipped[:].rearrange("p u c -> p c u"))
+            nc.vector.tensor_copy(out=grouped_words[:, bank_columns, :], in_=filled[b][:].rearrange("p u c -> p c u"))
         else:
-            nc.scalar.copy(out=grouped_words[:, bank_columns, :], in_=flipped[:].rearrange("p u c -> p c u"))
-    nc.vector.quantize_mx(out=codes.bitcast(FP8X4), scales=scales, in_=grouped[:])
+            nc.scalar.copy(out=grouped_words[:, bank_columns, :], in_=filled[b][:].rearrange("p u c -> p c u"))
+    return grouped
 
 
 def tile_gatedmemorymodule_pb_kernel(tc, queries, memory_items, wq, U_w, W_w, out_0, out_1):
@@ -53,25 +68,26 @@ def tile_gatedmemorymodule_pb_kernel(tc, queries, memory_items, wq, U_w, W_w, ou
 
     with ExitStack() as ctx:
         keep = ctx.enter_context(tc.tile_pool(name="keep", bufs=1))
-        query_pool = ctx.enter_context(tc.tile_pool(name="query", bufs=ROW_TILES // CHUNK))
+        query_pool = ctx.enter_context(tc.tile_pool(name="query", bufs=GROUPS // CHUNK_GROUPS))
         stage = ctx.enter_context(tc.tile_pool(name="stage", bufs=3))
-        packed = ctx.enter_context(tc.tile_pool(name="packed", bufs=8))
+        packed = ctx.enter_context(tc.tile_pool(name="packed", bufs=SCORE_LAG - QUANTISE_LAG + 2))
         stats = ctx.enter_context(tc.tile_pool(name="stats", bufs=4))
-        att_pool = ctx.enter_context(tc.tile_pool(name="att", bufs=4))
+        att_pool = ctx.enter_context(tc.tile_pool(name="att", bufs=6))
         banks = ctx.enter_context(tc.psum_pool(name="banks", bufs=4))
         logit_banks = ctx.enter_context(tc.psum_pool(name="logit_banks", bufs=3))
         clock_bank = ctx.enter_context(tc.psum_pool(name="clock_bank", bufs=1))
+        ctx.enter_context(tc.manual_schedule())
 
-        mem_raw = keep.tile([P, D], BF16)
-        nc.sync.dma_start(out=mem_raw[:], in_=memory_items)
-        wq_raw = keep.tile([P, D], BF16)
-        nc.sync.dma_start(out=wq_raw[:], in_=wq)
         u_raw = keep.tile([P, D // P, D], BF16)
         nc.sync.dma_start(out=u_raw[:], in_=U_w.rearrange("(i p) k -> p i k", p=P))
         w_raw = keep.tile([P, D // P, D], BF16)
         nc.sync.dma_start(out=w_raw[:], in_=W_w.rearrange("(i p) k -> p i k", p=P))
+        mem_raw = keep.tile([P, D], BF16)
+        nc.sync.dma_start(out=mem_raw[:], in_=memory_items)
+        wq_raw = keep.tile([P, D], BF16)
+        nc.sync.dma_start(out=wq_raw[:], in_=wq)
         query_chunks = []
-        for c in range(ROW_TILES // CHUNK):
+        for c in range(GROUPS // CHUNK_GROUPS):
             query_raw = query_pool.tile([P, CHUNK, D], BF16)
             nc.sync.dma_start(out=query_raw[:], in_=query_rows[:, c * CHUNK : (c + 1) * CHUNK, :])
             query_chunks.append(query_raw)
@@ -83,129 +99,202 @@ def tile_gatedmemorymodule_pb_kernel(tc, queries, memory_items, wq, U_w, W_w, ou
         scratch_out = keep.tile([P, 1], F32)
         nc.scalar.activation(out=scratch_out[:], in_=scratch_in[:], func=ACT.Exp)
 
-        slot_codes = keep.tile([P, 2 * SLOTS], U32, align_bytes=64)
-        slot_scales = keep.tile([P, 2 * SLOTS], U8, align_bytes=64)
-        transpose_and_quantise(
-            nc, banks, stage, identity[:], [mem_raw[:], wq_raw[:]], 0, GATE_COPY_EVERY, slot_codes[:], slot_scales[:]
-        )
         u_codes = keep.tile([P, D], U32, align_bytes=64)
         u_scales = keep.tile([P, D], U8, align_bytes=64)
-        transpose_and_quantise(
-            nc, banks, stage, identity[:], [u_raw[:, i, :] for i in range(D // P)], 1, GATE_COPY_EVERY, u_codes[:], u_scales[:]
+        u_grouped = gather_words(
+            nc, stage, flip_rows(nc, banks, identity[:], [u_raw[:, i, :] for i in range(D // P)]), 0, GATE_COPY_EVERY
         )
+        nc.vector.quantize_mx(out=u_codes[:].bitcast(FP8X4), scales=u_scales[:], in_=u_grouped[:])
         w_codes = keep.tile([P, D], U32, align_bytes=64)
         w_scales = keep.tile([P, D], U8, align_bytes=64)
-        transpose_and_quantise(
-            nc, banks, stage, identity[:], [w_raw[:, i, :] for i in range(D // P)], 1, GATE_COPY_EVERY, w_codes[:], w_scales[:]
+        w_grouped = gather_words(
+            nc, stage, flip_rows(nc, banks, identity[:], [w_raw[:, i, :] for i in range(D // P)]), 0, GATE_COPY_EVERY
         )
+        nc.vector.quantize_mx(out=w_codes[:].bitcast(FP8X4), scales=w_scales[:], in_=w_grouped[:])
+        slot_codes = keep.tile([P, 2 * SLOTS], U32, align_bytes=64)
+        slot_scales = keep.tile([P, 2 * SLOTS], U8, align_bytes=64)
+        slot_grouped = gather_words(
+            nc, stage, flip_rows(nc, banks, identity[:], [mem_raw[:], wq_raw[:]]), 1, GATE_COPY_EVERY
+        )
+        nc.vector.quantize_mx(out=slot_codes[:].bitcast(FP8X4), scales=slot_scales[:], in_=slot_grouped[:])
         slot_sum = keep.tile([P, D], F32)
         nc.vector.tensor_tensor(out=slot_sum[:], in0=wq_raw[:], in1=mem_raw[:], op=ALU.add)
         slot_diff = keep.tile([P, D], F32)
         nc.vector.tensor_tensor(out=slot_diff[:], in0=wq_raw[:], in1=mem_raw[:], op=ALU.subtract)
 
         gate_sum = logit_banks.tile([P, D], F32, tag="logits")
-        nc.tensor.matmul_mx(
-            out=gate_sum[:],
-            lhsT=slot_codes[:, 0:SLOTS].bitcast(FP8X4),
-            lhsT_scale=slot_scales[:, 0:SLOTS],
-            rhs=u_codes[:].bitcast(FP8X4),
-            rhs_scale=u_scales[:],
-            start=True,
-            stop=False,
-        )
-        nc.tensor.matmul_mx(
-            out=gate_sum[:],
-            lhsT=slot_codes[:, SLOTS : 2 * SLOTS].bitcast(FP8X4),
-            lhsT_scale=slot_scales[:, SLOTS : 2 * SLOTS],
-            rhs=w_codes[:].bitcast(FP8X4),
-            rhs_scale=w_scales[:],
-            start=False,
-            stop=True,
-        )
         tanh_half = keep.tile([P, D], F32)
-        nc.scalar.activation(out=tanh_half[:], in_=gate_sum[:], func=ACT.Tanh, scale=0.5)
         swing = keep.tile([P, D], F32)
-        nc.vector.scalar_tensor_tensor(
-            out=swing[:], in0=tanh_half[:], scalar=0.5, in1=slot_diff[:], op0=ALU.mult, op1=ALU.mult
-        )
         m_new = keep.tile([P, D], F32)
-        nc.vector.scalar_tensor_tensor(
-            out=m_new[:], in0=slot_sum[:], scalar=0.5, in1=swing[:], op0=ALU.mult, op1=ALU.add
-        )
-        nc.sync.dma_start(out=out_0, in_=m_new[:])
-
-        m_features = m_new[:].rearrange("s (u p e) -> s u e p", u=HALVES, e=2)
         m_flipped = logit_banks.tile([P, PACK, SLOTS], F32, tag="logits")
-        for u in range(HALVES):
-            for e in range(2):
-                nc.tensor.transpose(m_flipped[:, 2 * u + e, :], m_features[:, u, e, :], identity[:])
         m_grouped = keep.tile([P, SLOTS, PACK], BF16, align_bytes=64)
-        nc.vector.tensor_copy(out=m_grouped[:], in_=m_flipped[:].rearrange("p t s -> p s t"))
         m_codes = keep.tile([P, SLOTS], U32, align_bytes=64)
         m_scales = keep.tile([P, SLOTS], U8, align_bytes=64)
-        nc.vector.quantize_mx(
-            out=m_codes[:].bitcast(FP8X4), scales=m_scales[:], in_=m_grouped[:].rearrange("p s t -> p (s t)")
-        )
 
-        for c in range(ROW_TILES // CHUNK):
-            att = att_pool.tile([P, CHUNK, SLOTS], F32)
-            for first in range(0, CHUNK, GROUP):
-                query_codes = packed.tile([P, GROUP * P], U32, align_bytes=64)
-                query_scales = packed.tile([P, GROUP * P], U8, align_bytes=64)
-                transpose_and_quantise(
-                    nc,
-                    banks,
-                    stage,
-                    identity[:],
-                    [query_chunks[c][:, first + i, :] for i in range(GROUP)],
-                    (c * CHUNK + first) // BANK_TILES,
-                    QUERY_COPY_EVERY,
-                    query_codes[:],
-                    query_scales[:],
-                )
-                unread = clock_bank.tile([P, D], F32)
+        def gate_passes():
+            nc.tensor.matmul_mx(
+                out=gate_sum[:],
+                lhsT=slot_codes[:, 0:SLOTS].bitcast(FP8X4),
+                lhsT_scale=slot_scales[:, 0:SLOTS],
+                rhs=u_codes[:].bitcast(FP8X4),
+                rhs_scale=u_scales[:],
+                start=True,
+                stop=False,
+            )
+            nc.tensor.matmul_mx(
+                out=gate_sum[:],
+                lhsT=slot_codes[:, SLOTS : 2 * SLOTS].bitcast(FP8X4),
+                lhsT_scale=slot_scales[:, SLOTS : 2 * SLOTS],
+                rhs=w_codes[:].bitcast(FP8X4),
+                rhs_scale=w_scales[:],
+                start=False,
+                stop=True,
+            )
+
+        def gate_tanh():
+            nc.scalar.activation(out=tanh_half[:], in_=gate_sum[:], func=ACT.Tanh, scale=0.5)
+
+        def blend():
+            nc.vector.scalar_tensor_tensor(
+                out=swing[:], in0=tanh_half[:], scalar=0.5, in1=slot_diff[:], op0=ALU.mult, op1=ALU.mult
+            )
+            nc.vector.scalar_tensor_tensor(
+                out=m_new[:], in0=slot_sum[:], scalar=0.5, in1=swing[:], op0=ALU.mult, op1=ALU.add
+            )
+            nc.sync.dma_start(out=out_0, in_=m_new[:])
+
+        def flip_m_new():
+            m_features = m_new[:].rearrange("s (u p e) -> s u e p", u=HALVES, e=2)
+            for u in range(HALVES):
+                for e in range(2):
+                    nc.tensor.transpose(m_flipped[:, 2 * u + e, :], m_features[:, u, e, :], identity[:])
+
+        def quantise_m_new():
+            nc.vector.tensor_copy(out=m_grouped[:], in_=m_flipped[:].rearrange("p t s -> p s t"))
+            nc.vector.quantize_mx(
+                out=m_codes[:].bitcast(FP8X4), scales=m_scales[:], in_=m_grouped[:].rearrange("p s t -> p (s t)")
+            )
+
+        filled_of = {}
+        grouped_of = {}
+        codes_of = {}
+        scales_of = {}
+        logits_of = {}
+        max_of = {}
+        shift_of = {}
+        sum_of = {}
+        inverse_of = {}
+        att_of = {}
+
+        def flip(g):
+            first = (g % CHUNK_GROUPS) * GROUP
+            row_tiles = [query_chunks[g // CHUNK_GROUPS][:, first + i, :] for i in range(GROUP)]
+            filled_of[g] = flip_rows(nc, banks, identity[:], row_tiles)
+            unread = clock_bank.tile([P, D], F32)
+            nc.tensor.matmul_mx(
+                out=unread[:],
+                lhsT=slot_codes[:, 0:SLOTS].bitcast(FP8X4),
+                lhsT_scale=slot_scales[:, 0:SLOTS],
+                rhs=u_codes[:].bitcast(FP8X4),
+                rhs_scale=u_scales[:],
+                start=True,
+                stop=True,
+            )
+
+        def gather(g):
+            grouped_of[g] = gather_words(nc, stage, filled_of[g], g * GROUP // BANK_TILES, QUERY_COPY_EVERY)
+
+        def quantise(g):
+            query_codes = packed.tile([P, GROUP * P], U32, align_bytes=64)
+            query_scales = packed.tile([P, GROUP * P], U8, align_bytes=64)
+            nc.vector.quantize_mx(out=query_codes[:].bitcast(FP8X4), scales=query_scales[:], in_=grouped_of[g][:])
+            codes_of[g] = query_codes
+            scales_of[g] = query_scales
+
+        def score(g):
+            logits = logit_banks.tile([P, GROUP, SLOTS], F32, tag="logits")
+            for i in range(GROUP):
                 nc.tensor.matmul_mx(
-                    out=unread[:],
-                    lhsT=slot_codes[:, 0:SLOTS].bitcast(FP8X4),
-                    lhsT_scale=slot_scales[:, 0:SLOTS],
-                    rhs=u_codes[:].bitcast(FP8X4),
-                    rhs_scale=u_scales[:],
+                    out=logits[:, i, :],
+                    lhsT=codes_of[g][:, i * P : (i + 1) * P].bitcast(FP8X4),
+                    lhsT_scale=scales_of[g][:, i * P : (i + 1) * P],
+                    rhs=m_codes[:].bitcast(FP8X4),
+                    rhs_scale=m_scales[:],
                     start=True,
                     stop=True,
                 )
-                logits = logit_banks.tile([P, GROUP, SLOTS], F32, tag="logits")
-                for i in range(GROUP):
-                    nc.tensor.matmul_mx(
-                        out=logits[:, i, :],
-                        lhsT=query_codes[:, i * P : (i + 1) * P].bitcast(FP8X4),
-                        lhsT_scale=query_scales[:, i * P : (i + 1) * P],
-                        rhs=m_codes[:].bitcast(FP8X4),
-                        rhs_scale=m_scales[:],
-                        start=True,
-                        stop=True,
-                    )
-                row_max = stats.tile([P, GROUP], F32)
-                nc.vector.tensor_reduce(out=row_max[:], in_=logits[:], axis=AXIS.X, op=ALU.max)
-                shift = stats.tile([P, GROUP], F32)
-                nc.vector.tensor_scalar(out=shift[:], in0=row_max[:], scalar1=-INV_TEMP, scalar2=None, op0=ALU.mult)
-                row_sum = stats.tile([P, GROUP], F32)
-                for i in range(GROUP):
-                    nc.scalar.activation(
-                        out=att[:, first + i, :],
-                        in_=logits[:, i, :],
-                        func=ACT.Exp,
-                        bias=shift[:, i : i + 1],
-                        scale=INV_TEMP,
-                        accum_out=row_sum[:, i : i + 1],
-                    )
-                inv_sum = stats.tile([P, GROUP], F32)
-                nc.vector.reciprocal(out=inv_sum[:], in_=row_sum[:])
-                for i in range(GROUP):
-                    nc.vector.tensor_scalar(
-                        out=att[:, first + i, :],
-                        in0=att[:, first + i, :],
-                        scalar1=inv_sum[:, i : i + 1],
-                        scalar2=None,
-                        op0=ALU.mult,
-                    )
-            nc.sync.dma_start(out=att_rows[:, c * CHUNK : (c + 1) * CHUNK, :], in_=att[:])
+            logits_of[g] = logits
+
+        def find_max(g):
+            row_max = stats.tile([P, GROUP], F32)
+            nc.vector.tensor_reduce(out=row_max[:], in_=logits_of[g][:], axis=AXIS.X, op=ALU.max)
+            max_of[g] = row_max
+
+        def make_shift(g):
+            shift = stats.tile([P, GROUP], F32)
+            nc.vector.tensor_scalar(out=shift[:], in0=max_of[g][:], scalar1=-INV_TEMP, scalar2=None, op0=ALU.mult)
+            shift_of[g] = shift
+
+        def exponentials(g):
+            if g % CHUNK_GROUPS == 0:
+                att = att_pool.tile([P, CHUNK, SLOTS], F32)
+                att_of[g // CHUNK_GROUPS] = att
+            first = (g % CHUNK_GROUPS) * GROUP
+            row_sum = stats.tile([P, GROUP], F32)
+            for i in range(GROUP):
+                nc.scalar.activation(
+                    out=att_of[g // CHUNK_GROUPS][:, first + i, :],
+                    in_=logits_of[g][:, i, :],
+                    func=ACT.Exp,
+                    bias=shift_of[g][:, i : i + 1],
+                    scale=INV_TEMP,
+                    accum_out=row_sum[:, i : i + 1],
+                )
+            sum_of[g] = row_sum
+
+        def invert_sums(g):
+            inverse = stats.tile([P, GROUP], F32)
+            nc.vector.reciprocal(out=inverse[:], in_=sum_of[g][:])
+            inverse_of[g] = inverse
+
+        def normalise(g):
+            c = g // CHUNK_GROUPS
+            first = (g % CHUNK_GROUPS) * GROUP
+            for i in range(GROUP):
+                nc.vector.tensor_scalar(
+                    out=att_of[c][:, first + i, :],
+                    in0=att_of[c][:, first + i, :],
+                    scalar1=inverse_of[g][:, i : i + 1],
+                    scalar2=None,
+                    op0=ALU.mult,
+                )
+            if g % CHUNK_GROUPS == CHUNK_GROUPS - 1:
+                nc.sync.dma_start(out=att_rows[:, c * CHUNK : (c + 1) * CHUNK, :], in_=att_of[c][:])
+
+        def run(stage_of_pipeline, g):
+            if 0 <= g < GROUPS:
+                stage_of_pipeline(g)
+
+        def step(s):
+            run(flip, s)
+            run(score, s - SCORE_LAG)
+            run(find_max, s - MAX_LAG)
+            run(invert_sums, s - NORMALISE_LAG)
+            run(quantise, s - QUANTISE_LAG)
+            run(make_shift, s - MAX_LAG)
+            run(normalise, s - NORMALISE_LAG)
+            run(gather, s - GATHER_LAG)
+            run(exponentials, s - EXP_LAG)
+
+        step(0)
+        gate_passes()
+        step(1)
+        gate_tanh()
+        step(2)
+        blend()
+        step(3)
+        flip_m_new()
+        step(4)
+        quantise_m_new()
+        for s in range(5, GROUPS + NORMALISE_LAG):
+            step(s)

@@ -29,7 +29,7 @@ QUERY_COPY_EVERY = 6
 
 GATHER_LAG = 1
 QUANTISE_LAG = 2
-SCORE_LAG = 6
+SCORE_LAG = 3
 MAX_LAG = SCORE_LAG + 1
 EXP_LAG = SCORE_LAG + 2
 NORMALISE_LAG = SCORE_LAG + 3
@@ -72,24 +72,30 @@ def tile_gatedmemorymodule_pb_kernel(tc, queries, memory_items, wq, U_w, W_w, ou
         stage = ctx.enter_context(tc.tile_pool(name="stage", bufs=3))
         packed = ctx.enter_context(tc.tile_pool(name="packed", bufs=SCORE_LAG - QUANTISE_LAG + 2))
         stats = ctx.enter_context(tc.tile_pool(name="stats", bufs=4))
-        att_pool = ctx.enter_context(tc.tile_pool(name="att", bufs=6))
+        att_pool = ctx.enter_context(tc.tile_pool(name="att", bufs=10))
         banks = ctx.enter_context(tc.psum_pool(name="banks", bufs=4))
         logit_banks = ctx.enter_context(tc.psum_pool(name="logit_banks", bufs=3))
         clock_bank = ctx.enter_context(tc.psum_pool(name="clock_bank", bufs=1))
         ctx.enter_context(tc.manual_schedule())
 
-        u_raw = keep.tile([P, D // P, D], BF16)
-        nc.sync.dma_start(out=u_raw[:], in_=U_w.rearrange("(i p) k -> p i k", p=P))
-        w_raw = keep.tile([P, D // P, D], BF16)
-        nc.sync.dma_start(out=w_raw[:], in_=W_w.rearrange("(i p) k -> p i k", p=P))
         mem_raw = keep.tile([P, D], BF16)
         nc.sync.dma_start(out=mem_raw[:], in_=memory_items)
         wq_raw = keep.tile([P, D], BF16)
         nc.sync.dma_start(out=wq_raw[:], in_=wq)
+        u_raw = keep.tile([P, D // P, D], BF16)
+        nc.sync.dma_start(out=u_raw[:], in_=U_w.rearrange("(i p) k -> p i k", p=P))
+        w_raw = keep.tile([P, D // P, D], BF16)
+        nc.sync.dma_start(out=w_raw[:], in_=W_w.rearrange("(i p) k -> p i k", p=P))
         query_chunks = []
         for c in range(GROUPS // CHUNK_GROUPS):
             query_raw = query_pool.tile([P, CHUNK, D], BF16)
-            nc.sync.dma_start(out=query_raw[:], in_=query_rows[:, c * CHUNK : (c + 1) * CHUNK, :])
+            loads = CHUNK_GROUPS if c == 0 else 1
+            tiles = CHUNK // loads
+            for i in range(loads):
+                nc.sync.dma_start(
+                    out=query_raw[:, i * tiles : (i + 1) * tiles, :],
+                    in_=query_rows[:, c * CHUNK + i * tiles : c * CHUNK + (i + 1) * tiles, :],
+                )
             query_chunks.append(query_raw)
 
         identity = keep.tile([P, P], F32)
@@ -99,6 +105,12 @@ def tile_gatedmemorymodule_pb_kernel(tc, queries, memory_items, wq, U_w, W_w, ou
         scratch_out = keep.tile([P, 1], F32)
         nc.scalar.activation(out=scratch_out[:], in_=scratch_in[:], func=ACT.Exp)
 
+        slot_codes = keep.tile([P, 2 * SLOTS], U32, align_bytes=64)
+        slot_scales = keep.tile([P, 2 * SLOTS], U8, align_bytes=64)
+        slot_grouped = gather_words(
+            nc, stage, flip_rows(nc, banks, identity[:], [mem_raw[:], wq_raw[:]]), 1, GATE_COPY_EVERY
+        )
+        nc.vector.quantize_mx(out=slot_codes[:].bitcast(FP8X4), scales=slot_scales[:], in_=slot_grouped[:])
         u_codes = keep.tile([P, D], U32, align_bytes=64)
         u_scales = keep.tile([P, D], U8, align_bytes=64)
         u_grouped = gather_words(
@@ -111,12 +123,6 @@ def tile_gatedmemorymodule_pb_kernel(tc, queries, memory_items, wq, U_w, W_w, ou
             nc, stage, flip_rows(nc, banks, identity[:], [w_raw[:, i, :] for i in range(D // P)]), 0, GATE_COPY_EVERY
         )
         nc.vector.quantize_mx(out=w_codes[:].bitcast(FP8X4), scales=w_scales[:], in_=w_grouped[:])
-        slot_codes = keep.tile([P, 2 * SLOTS], U32, align_bytes=64)
-        slot_scales = keep.tile([P, 2 * SLOTS], U8, align_bytes=64)
-        slot_grouped = gather_words(
-            nc, stage, flip_rows(nc, banks, identity[:], [mem_raw[:], wq_raw[:]]), 1, GATE_COPY_EVERY
-        )
-        nc.vector.quantize_mx(out=slot_codes[:].bitcast(FP8X4), scales=slot_scales[:], in_=slot_grouped[:])
         slot_sum = keep.tile([P, D], F32)
         nc.vector.tensor_tensor(out=slot_sum[:], in0=wq_raw[:], in1=mem_raw[:], op=ALU.add)
         slot_diff = keep.tile([P, D], F32)
@@ -232,7 +238,9 @@ def tile_gatedmemorymodule_pb_kernel(tc, queries, memory_items, wq, U_w, W_w, ou
 
         def make_shift(g):
             shift = stats.tile([P, GROUP], F32)
-            nc.vector.tensor_scalar(out=shift[:], in0=max_of[g][:], scalar1=-INV_TEMP, scalar2=None, op0=ALU.mult)
+            nc.gpsimd.tensor_scalar(
+                out=shift[:], in0=max_of[g][:], scalar1=-INV_TEMP, scalar2=0.0, op0=ALU.mult, op1=ALU.add
+            )
             shift_of[g] = shift
 
         def exponentials(g):
@@ -279,22 +287,20 @@ def tile_gatedmemorymodule_pb_kernel(tc, queries, memory_items, wq, U_w, W_w, ou
             run(flip, s)
             run(score, s - SCORE_LAG)
             run(find_max, s - MAX_LAG)
+            run(gather, s - GATHER_LAG)
             run(invert_sums, s - NORMALISE_LAG)
             run(quantise, s - QUANTISE_LAG)
             run(make_shift, s - MAX_LAG)
             run(normalise, s - NORMALISE_LAG)
-            run(gather, s - GATHER_LAG)
             run(exponentials, s - EXP_LAG)
 
         step(0)
         gate_passes()
         step(1)
         gate_tanh()
-        step(2)
         blend()
-        step(3)
+        step(2)
         flip_m_new()
-        step(4)
         quantise_m_new()
-        for s in range(5, GROUPS + NORMALISE_LAG):
+        for s in range(3, GROUPS + NORMALISE_LAG):
             step(s)

@@ -24,6 +24,7 @@ GROUP = 4
 CHUNK = 8
 GROUPS = ROWS // P // GROUP
 CHUNK_GROUPS = CHUNK // GROUP
+FINE_CHUNKS = 2
 GATE_COPY_EVERY = 2
 QUERY_COPY_EVERY = 6
 
@@ -75,7 +76,6 @@ def tile_gatedmemorymodule_pb_kernel(tc, queries, memory_items, wq, U_w, W_w, ou
         att_pool = ctx.enter_context(tc.tile_pool(name="att", bufs=10))
         banks = ctx.enter_context(tc.psum_pool(name="banks", bufs=4))
         logit_banks = ctx.enter_context(tc.psum_pool(name="logit_banks", bufs=3))
-        clock_bank = ctx.enter_context(tc.psum_pool(name="clock_bank", bufs=1))
         ctx.enter_context(tc.manual_schedule())
 
         mem_raw = keep.tile([P, D], BF16)
@@ -105,6 +105,10 @@ def tile_gatedmemorymodule_pb_kernel(tc, queries, memory_items, wq, U_w, W_w, ou
         scratch_out = keep.tile([P, 1], F32)
         nc.scalar.activation(out=scratch_out[:], in_=scratch_in[:], func=ACT.Exp)
 
+        slot_sum = keep.tile([P, D], F32)
+        nc.vector.tensor_tensor(out=slot_sum[:], in0=wq_raw[:], in1=mem_raw[:], op=ALU.add)
+        slot_diff = keep.tile([P, D], F32)
+        nc.vector.tensor_tensor(out=slot_diff[:], in0=wq_raw[:], in1=mem_raw[:], op=ALU.subtract)
         slot_codes = keep.tile([P, 2 * SLOTS], U32, align_bytes=64)
         slot_scales = keep.tile([P, 2 * SLOTS], U8, align_bytes=64)
         slot_grouped = gather_words(
@@ -123,10 +127,6 @@ def tile_gatedmemorymodule_pb_kernel(tc, queries, memory_items, wq, U_w, W_w, ou
             nc, stage, flip_rows(nc, banks, identity[:], [w_raw[:, i, :] for i in range(D // P)]), 0, GATE_COPY_EVERY
         )
         nc.vector.quantize_mx(out=w_codes[:].bitcast(FP8X4), scales=w_scales[:], in_=w_grouped[:])
-        slot_sum = keep.tile([P, D], F32)
-        nc.vector.tensor_tensor(out=slot_sum[:], in0=wq_raw[:], in1=mem_raw[:], op=ALU.add)
-        slot_diff = keep.tile([P, D], F32)
-        nc.vector.tensor_tensor(out=slot_diff[:], in0=wq_raw[:], in1=mem_raw[:], op=ALU.subtract)
 
         gate_sum = logit_banks.tile([P, D], F32, tag="logits")
         tanh_half = keep.tile([P, D], F32)
@@ -196,16 +196,6 @@ def tile_gatedmemorymodule_pb_kernel(tc, queries, memory_items, wq, U_w, W_w, ou
             first = (g % CHUNK_GROUPS) * GROUP
             row_tiles = [query_chunks[g // CHUNK_GROUPS][:, first + i, :] for i in range(GROUP)]
             filled_of[g] = flip_rows(nc, banks, identity[:], row_tiles)
-            unread = clock_bank.tile([P, D], F32)
-            nc.tensor.matmul_mx(
-                out=unread[:],
-                lhsT=slot_codes[:, 0:SLOTS].bitcast(FP8X4),
-                lhsT_scale=slot_scales[:, 0:SLOTS],
-                rhs=u_codes[:].bitcast(FP8X4),
-                rhs_scale=u_scales[:],
-                start=True,
-                stop=True,
-            )
 
         def gather(g):
             grouped_of[g] = gather_words(nc, stage, filled_of[g], g * GROUP // BANK_TILES, QUERY_COPY_EVERY)
@@ -276,7 +266,10 @@ def tile_gatedmemorymodule_pb_kernel(tc, queries, memory_items, wq, U_w, W_w, ou
                     scalar2=None,
                     op0=ALU.mult,
                 )
-            if g % CHUNK_GROUPS == CHUNK_GROUPS - 1:
+            if c >= GROUPS // CHUNK_GROUPS - FINE_CHUNKS:
+                rows = slice(c * CHUNK + first, c * CHUNK + first + GROUP)
+                nc.sync.dma_start(out=att_rows[:, rows, :], in_=att_of[c][:, first : first + GROUP, :])
+            elif g % CHUNK_GROUPS == CHUNK_GROUPS - 1:
                 nc.sync.dma_start(out=att_rows[:, c * CHUNK : (c + 1) * CHUNK, :], in_=att_of[c][:])
 
         def run(stage_of_pipeline, g):

@@ -33,7 +33,9 @@ QUANTISE_LAG = 2
 SCORE_LAG = 3
 MAX_LAG = SCORE_LAG + 1
 EXP_LAG = SCORE_LAG + 2
-NORMALISE_LAG = SCORE_LAG + 3
+INVERT_LAG = SCORE_LAG + 3
+NORMALISE_LAG = SCORE_LAG + 4
+GPSIMD_TILES = 1
 
 FLOPS = 2 * (2 * SLOTS * D * D + ROWS * D * SLOTS)
 
@@ -255,10 +257,23 @@ def tile_gatedmemorymodule_pb_kernel(tc, queries, memory_items, wq, U_w, W_w, ou
             nc.vector.reciprocal(out=inverse[:], in_=sum_of[g][:])
             inverse_of[g] = inverse
 
+        def normalise_on_gpsimd(g):
+            c = g // CHUNK_GROUPS
+            first = (g % CHUNK_GROUPS) * GROUP
+            for i in range(GROUP - GPSIMD_TILES, GROUP):
+                nc.gpsimd.tensor_scalar(
+                    out=att_of[c][:, first + i, :],
+                    in0=att_of[c][:, first + i, :],
+                    scalar1=inverse_of[g][:, i : i + 1],
+                    scalar2=0.0,
+                    op0=ALU.mult,
+                    op1=ALU.add,
+                )
+
         def normalise(g):
             c = g // CHUNK_GROUPS
             first = (g % CHUNK_GROUPS) * GROUP
-            for i in range(GROUP):
+            for i in range(GROUP - GPSIMD_TILES):
                 nc.vector.tensor_scalar(
                     out=att_of[c][:, first + i, :],
                     in0=att_of[c][:, first + i, :],
@@ -281,10 +296,11 @@ def tile_gatedmemorymodule_pb_kernel(tc, queries, memory_items, wq, U_w, W_w, ou
             run(score, s - SCORE_LAG)
             run(find_max, s - MAX_LAG)
             run(gather, s - GATHER_LAG)
-            run(invert_sums, s - NORMALISE_LAG)
             run(quantise, s - QUANTISE_LAG)
             run(make_shift, s - MAX_LAG)
             run(normalise, s - NORMALISE_LAG)
+            run(invert_sums, s - INVERT_LAG)
+            run(normalise_on_gpsimd, s - INVERT_LAG)
             run(exponentials, s - EXP_LAG)
 
         step(0)

@@ -30,7 +30,7 @@ QUERY_COPY_EVERY = 6
 
 GATHER_LAG = 1
 QUANTISE_LAG = 2
-SCORE_LAG = 3
+SCORE_LAG = 4
 MAX_LAG = SCORE_LAG + 1
 EXP_LAG = SCORE_LAG + 2
 INVERT_LAG = SCORE_LAG + 3

@@ -26,7 +26,7 @@ GROUPS = ROWS // P // GROUP
 CHUNK_GROUPS = CHUNK // GROUP
 FINE_CHUNKS = 2
 GATE_COPY_EVERY = 2
-QUERY_COPY_EVERY = 6
+QUERY_COPY_EVERY = 8
 
 GATHER_LAG = 1
 QUANTISE_LAG = 2

@@ -72,12 +72,12 @@ def tile_gatedmemorymodule_pb_kernel(tc, queries, memory_items, wq, U_w, W_w, ou
     with ExitStack() as ctx:
         keep = ctx.enter_context(tc.tile_pool(name="keep", bufs=1))
         query_pool = ctx.enter_context(tc.tile_pool(name="query", bufs=GROUPS // CHUNK_GROUPS))
-        stage = ctx.enter_context(tc.tile_pool(name="stage", bufs=3))
-        packed = ctx.enter_context(tc.tile_pool(name="packed", bufs=SCORE_LAG - QUANTISE_LAG + 2))
-        stats = ctx.enter_context(tc.tile_pool(name="stats", bufs=4))
+        stage = ctx.enter_context(tc.tile_pool(name="stage", bufs=4))
+        packed = ctx.enter_context(tc.tile_pool(name="packed", bufs=SCORE_LAG - QUANTISE_LAG + 3))
+        stats = ctx.enter_context(tc.tile_pool(name="stats", bufs=6))
         att_pool = ctx.enter_context(tc.tile_pool(name="att", bufs=10))
         banks = ctx.enter_context(tc.psum_pool(name="banks", bufs=4))
-        logit_banks = ctx.enter_context(tc.psum_pool(name="logit_banks", bufs=3))
+        logit_banks = ctx.enter_context(tc.psum_pool(name="logit_banks", bufs=4))
         ctx.enter_context(tc.manual_schedule())
 
         mem_raw = keep.tile([P, D], BF16)

from contextlib import ExitStack

import concourse.mybir as mybir
from concourse.masks import make_identity

F32 = mybir.dt.float32
BF16 = mybir.dt.bfloat16
U32 = mybir.dt.uint32
U8 = mybir.dt.uint8
FP8X4 = mybir.dt.float8_e4m3fn_x4
ACT = mybir.ActivationFunctionType
ALU = mybir.AluOpType
AXIS = mybir.AxisListType

P = 128
D = 512
SLOTS = 128
ROWS = 128 * 128
INV_TEMP = 1.0 / 0.1
PACK = 4
HALVES = 2
BANK_TILES = 2
GROUP = 4
CHUNK = 8
GROUPS = ROWS // P // GROUP
CHUNK_GROUPS = CHUNK // GROUP
FINE_CHUNKS = 2
GATE_COPY_EVERY = 2
QUERY_COPY_EVERY = 8

GATHER_LAG = 1
QUANTISE_LAG = 2
SCORE_LAG = 4
MAX_LAG = SCORE_LAG + 1
EXP_LAG = SCORE_LAG + 2
INVERT_LAG = SCORE_LAG + 3
NORMALISE_LAG = SCORE_LAG + 4
GPSIMD_TILES = 1

FLOPS = 2 * (2 * SLOTS * D * D + ROWS * D * SLOTS)


def flip_rows(nc, banks, identity, row_tiles):
    filled = []
    for b in range(len(row_tiles) // BANK_TILES):
        flipped = banks.tile([P, HALVES, BANK_TILES * P], F32, tag="flipped")
        for i in range(BANK_TILES):
            words = row_tiles[b * BANK_TILES + i].bitcast(F32)
            for u in range(HALVES):
                nc.tensor.transpose(flipped[:, u, i * P : (i + 1) * P], words[:, u * P : (u + 1) * P], identity)
        filled.append(flipped)
    return filled


def gather_words(nc, stage, filled, first_bank, vector_every):
    grouped = stage.tile([P, len(filled) * BANK_TILES * P * PACK], BF16, tag="grouped", align_bytes=64)
    grouped_words = grouped[:].bitcast(F32).rearrange("p (c u) -> p c u", u=HALVES)
    for b in range(len(filled)):
        bank_columns = slice(b * BANK_TILES * P, (b + 1) * BANK_TILES * P)
        if (first_bank + b) % vector_every == 0:
            nc.vector.tensor_copy(out=grouped_words[:, bank_columns, :], in_=filled[b][:].rearrange("p u c -> p c u"))
        else:
            nc.scalar.copy(out=grouped_words[:, bank_columns, :], in_=filled[b][:].rearrange("p u c -> p c u"))
    return grouped


def tile_gatedmemorymodule_pb_kernel(tc, queries, memory_items, wq, U_w, W_w, out_0, out_1):
    nc = tc.nc
    query_rows = queries.flatten_outer_dims().rearrange("(p t) d -> p t d", p=P)
    att_rows = out_1.flatten_outer_dims().rearrange("(p t) m -> p t m", p=P)

    with ExitStack() as ctx:
        keep = ctx.enter_context(tc.tile_pool(name="keep", bufs=1))
        query_pool = ctx.enter_context(tc.tile_pool(name="query", bufs=GROUPS // CHUNK_GROUPS))
        stage = ctx.enter_context(tc.tile_pool(name="stage", bufs=4))
        packed = ctx.enter_context(tc.tile_pool(name="packed", bufs=SCORE_LAG - QUANTISE_LAG + 3))
        stats = ctx.enter_context(tc.tile_pool(name="stats", bufs=6))
        att_pool = ctx.enter_context(tc.tile_pool(name="att", bufs=10))
        banks = ctx.enter_context(tc.psum_pool(name="banks", bufs=4))
        logit_banks = ctx.enter_context(tc.psum_pool(name="logit_banks", bufs=4))
        ctx.enter_context(tc.manual_schedule())

        mem_raw = keep.tile([P, D], BF16)
        nc.sync.dma_start(out=mem_raw[:], in_=memory_items)
        wq_raw = keep.tile([P, D], BF16)
        nc.sync.dma_start(out=wq_raw[:], in_=wq)
        u_raw = keep.tile([P, D // P, D], BF16)
        nc.sync.dma_start(out=u_raw[:], in_=U_w.rearrange("(i p) k -> p i k", p=P))
        w_raw = keep.tile([P, D // P, D], BF16)
        nc.sync.dma_start(out=w_raw[:], in_=W_w.rearrange("(i p) k -> p i k", p=P))
        query_chunks = []
        for c in range(GROUPS // CHUNK_GROUPS):
            query_raw = query_pool.tile([P, CHUNK, D], BF16)
            loads = CHUNK_GROUPS if c == 0 else 1
            tiles = CHUNK // loads
            for i in range(loads):
                nc.sync.dma_start(
                    out=query_raw[:, i * tiles : (i + 1) * tiles, :],
                    in_=query_rows[:, c * CHUNK + i * tiles : c * CHUNK + (i + 1) * tiles, :],
                )
            query_chunks.append(query_raw)

        identity = keep.tile([P, P], F32)
        make_identity(nc, identity[:])
        scratch_in = keep.tile([P, 1], F32)
        nc.vector.memset(scratch_in[:], 0.0)
        scratch_out = keep.tile([P, 1], F32)
        nc.scalar.activation(out=scratch_out[:], in_=scratch_in[:], func=ACT.Exp)

        slot_sum = keep.tile([P, D], F32)
        nc.vector.tensor_tensor(out=slot_sum[:], in0=wq_raw[:], in1=mem_raw[:], op=ALU.add)
        slot_diff = keep.tile([P, D], F32)
        nc.vector.tensor_tensor(out=slot_diff[:], in0=wq_raw[:], in1=mem_raw[:], op=ALU.subtract)
        slot_codes = keep.tile([P, 2 * SLOTS], U32, align_bytes=64)
        slot_scales = keep.tile([P, 2 * SLOTS], U8, align_bytes=64)
        slot_grouped = gather_words(
            nc, stage, flip_rows(nc, banks, identity[:], [mem_raw[:], wq_raw[:]]), 1, GATE_COPY_EVERY
        )
        nc.vector.quantize_mx(out=slot_codes[:].bitcast(FP8X4), scales=slot_scales[:], in_=slot_grouped[:])
        u_codes = keep.tile([P, D], U32, align_bytes=64)
        u_scales = keep.tile([P, D], U8, align_bytes=64)
        u_grouped = gather_words(
            nc, stage, flip_rows(nc, banks, identity[:], [u_raw[:, i, :] for i in range(D // P)]), 0, GATE_COPY_EVERY
        )
        nc.vector.quantize_mx(out=u_codes[:].bitcast(FP8X4), scales=u_scales[:], in_=u_grouped[:])
        w_codes = keep.tile([P, D], U32, align_bytes=64)
        w_scales = keep.tile([P, D], U8, align_bytes=64)
        w_grouped = gather_words(
            nc, stage, flip_rows(nc, banks, identity[:], [w_raw[:, i, :] for i in range(D // P)]), 0, GATE_COPY_EVERY
        )
        nc.vector.quantize_mx(out=w_codes[:].bitcast(FP8X4), scales=w_scales[:], in_=w_grouped[:])

        gate_sum = logit_banks.tile([P, D], F32, tag="logits")
        tanh_half = keep.tile([P, D], F32)
        swing = keep.tile([P, D], F32)
        m_new = keep.tile([P, D], F32)
        m_flipped = logit_banks.tile([P, PACK, SLOTS], F32, tag="logits")
        m_grouped = keep.tile([P, SLOTS, PACK], BF16, align_bytes=64)
        m_codes = keep.tile([P, SLOTS], U32, align_bytes=64)
        m_scales = keep.tile([P, SLOTS], U8, align_bytes=64)

        def gate_passes():
            nc.tensor.matmul_mx(
                out=gate_sum[:],
                lhsT=slot_codes[:, 0:SLOTS].bitcast(FP8X4),
                lhsT_scale=slot_scales[:, 0:SLOTS],
                rhs=u_codes[:].bitcast(FP8X4),
                rhs_scale=u_scales[:],
                start=True,
                stop=False,
            )
            nc.tensor.matmul_mx(
                out=gate_sum[:],
                lhsT=slot_codes[:, SLOTS : 2 * SLOTS].bitcast(FP8X4),
                lhsT_scale=slot_scales[:, SLOTS : 2 * SLOTS],
                rhs=w_codes[:].bitcast(FP8X4),
                rhs_scale=w_scales[:],
                start=False,
                stop=True,
            )

        def gate_tanh():
            nc.scalar.activation(out=tanh_half[:], in_=gate_sum[:], func=ACT.Tanh, scale=0.5)

        def blend():
            nc.vector.scalar_tensor_tensor(
                out=swing[:], in0=tanh_half[:], scalar=0.5, in1=slot_diff[:], op0=ALU.mult, op1=ALU.mult
            )
            nc.vector.scalar_tensor_tensor(
                out=m_new[:], in0=slot_sum[:], scalar=0.5, in1=swing[:], op0=ALU.mult, op1=ALU.add
            )
            nc.sync.dma_start(out=out_0, in_=m_new[:])

        def flip_m_new():
            m_features = m_new[:].rearrange("s (u p e) -> s u e p", u=HALVES, e=2)
            for u in range(HALVES):
                for e in range(2):
                    nc.tensor.transpose(m_flipped[:, 2 * u + e, :], m_features[:, u, e, :], identity[:])

        def quantise_m_new():
            nc.vector.tensor_copy(out=m_grouped[:], in_=m_flipped[:].rearrange("p t s -> p s t"))
            nc.vector.quantize_mx(
                out=m_codes[:].bitcast(FP8X4), scales=m_scales[:], in_=m_grouped[:].rearrange("p s t -> p (s t)")
            )

        filled_of = {}
        grouped_of = {}
        codes_of = {}
        scales_of = {}
        logits_of = {}
        max_of = {}
        shift_of = {}
        sum_of = {}
        inverse_of = {}
        att_of = {}

        def flip(g):
            first = (g % CHUNK_GROUPS) * GROUP
            row_tiles = [query_chunks[g // CHUNK_GROUPS][:, first + i, :] for i in range(GROUP)]
            filled_of[g] = flip_rows(nc, banks, identity[:], row_tiles)

        def gather(g):
            grouped_of[g] = gather_words(nc, stage, filled_of[g], g * GROUP // BANK_TILES, QUERY_COPY_EVERY)

        def quantise(g):
            query_codes = packed.tile([P, GROUP * P], U32, align_bytes=64)
            query_scales = packed.tile([P, GROUP * P], U8, align_bytes=64)
            nc.vector.quantize_mx(out=query_codes[:].bitcast(FP8X4), scales=query_scales[:], in_=grouped_of[g][:])
            codes_of[g] = query_codes
            scales_of[g] = query_scales

        def score(g):
            logits = logit_banks.tile([P, GROUP, SLOTS], F32, tag="logits")
            for i in range(GROUP):
                nc.tensor.matmul_mx(
                    out=logits[:, i, :],
                    lhsT=codes_of[g][:, i * P : (i + 1) * P].bitcast(FP8X4),
                    lhsT_scale=scales_of[g][:, i * P : (i + 1) * P],
                    rhs=m_codes[:].bitcast(FP8X4),
                    rhs_scale=m_scales[:],
                    start=True,
                    stop=True,
                )
            logits_of[g] = logits

        def find_max(g):
            row_max = stats.tile([P, GROUP], F32)
            nc.vector.tensor_reduce(out=row_max[:], in_=logits_of[g][:], axis=AXIS.X, op=ALU.max)
            max_of[g] = row_max

        def make_shift(g):
            shift = stats.tile([P, GROUP], F32)
            nc.gpsimd.tensor_scalar(
                out=shift[:], in0=max_of[g][:], scalar1=-INV_TEMP, scalar2=0.0, op0=ALU.mult, op1=ALU.add
            )
            shift_of[g] = shift

        def exponentials(g):
            if g % CHUNK_GROUPS == 0:
                att = att_pool.tile([P, CHUNK, SLOTS], F32)
                att_of[g // CHUNK_GROUPS] = att
            first = (g % CHUNK_GROUPS) * GROUP
            row_sum = stats.tile([P, GROUP], F32)
            for i in range(GROUP):
                nc.scalar.activation(
                    out=att_of[g // CHUNK_GROUPS][:, first + i, :],
                    in_=logits_of[g][:, i, :],
                    func=ACT.Exp,
                    bias=shift_of[g][:, i : i + 1],
                    scale=INV_TEMP,
                    accum_out=row_sum[:, i : i + 1],
                )
            sum_of[g] = row_sum

        def invert_sums(g):
            inverse = stats.tile([P, GROUP], F32)
            nc.vector.reciprocal(out=inverse[:], in_=sum_of[g][:])
            inverse_of[g] = inverse

        def normalise_on_gpsimd(g):
            c = g // CHUNK_GROUPS
            first = (g % CHUNK_GROUPS) * GROUP
            for i in range(GROUP - GPSIMD_TILES, GROUP):
                nc.gpsimd.tensor_scalar(
                    out=att_of[c][:, first + i, :],
                    in0=att_of[c][:, first + i, :],
                    scalar1=inverse_of[g][:, i : i + 1],
                    scalar2=0.0,
                    op0=ALU.mult,
                    op1=ALU.add,
                )

        def normalise(g):
            c = g // CHUNK_GROUPS
            first = (g % CHUNK_GROUPS) * GROUP
            for i in range(GROUP - GPSIMD_TILES):
                nc.vector.tensor_scalar(
                    out=att_of[c][:, first + i, :],
                    in0=att_of[c][:, first + i, :],
                    scalar1=inverse_of[g][:, i : i + 1],
                    scalar2=None,
                    op0=ALU.mult,
                )
            if c >= GROUPS // CHUNK_GROUPS - FINE_CHUNKS:
                rows = slice(c * CHUNK + first, c * CHUNK + first + GROUP)
                nc.sync.dma_start(out=att_rows[:, rows, :], in_=att_of[c][:, first : first + GROUP, :])
            elif g % CHUNK_GROUPS == CHUNK_GROUPS - 1:
                nc.sync.dma_start(out=att_rows[:, c * CHUNK : (c + 1) * CHUNK, :], in_=att_of[c][:])

        def run(stage_of_pipeline, g):
            if 0 <= g < GROUPS:
                stage_of_pipeline(g)

        def step(s):
            run(flip, s)
            run(score, s - SCORE_LAG)
            run(find_max, s - MAX_LAG)
            run(gather, s - GATHER_LAG)
            run(quantise, s - QUANTISE_LAG)
            run(make_shift, s - MAX_LAG)
            run(normalise, s - NORMALISE_LAG)
            run(invert_sums, s - INVERT_LAG)
            run(normalise_on_gpsimd, s - INVERT_LAG)
            run(exponentials, s - EXP_LAG)

        step(0)
        gate_passes()
        step(1)
        gate_tanh()
        blend()
        step(2)
        flip_m_new()
        quantise_m_new()
        for s in range(3, GROUPS + NORMALISE_LAG):
            step(s)
